import numpy as np
import ml_dtypes


def mxq(x, axis, fmt="e4m3"):
    dtype, down = {"e4m3": (ml_dtypes.float8_e4m3fn, 7), "e5m2": (ml_dtypes.float8_e5m2, 14)}[fmt]
    v = np.moveaxis(np.asarray(x, np.float32).astype(ml_dtypes.bfloat16).astype(np.float64), axis, -1)
    blocks = v.reshape(v.shape[:-1] + (-1, 32))
    amax = np.abs(blocks).max(-1, keepdims=True)
    byte = np.maximum(np.where(amax > 0, np.frexp(amax)[1] - 1 + 127, 0) - down, 1)
    scale = np.exp2(byte - 127.0)
    codes = (blocks / scale).astype(np.float32).astype(dtype).astype(np.float64)
    return np.moveaxis((codes * scale).reshape(v.shape), -1, axis)


WIDE = False


def mx_kscale(k):
    if not WIDE:
        return np.ones(k)
    levels = np.array([10, -10, 5, -5, 0])
    a = np.random.permutation(np.resize(levels, k // 512 * 4)).reshape(k // 512, 4)
    idx = np.arange(k)
    return np.exp2(a[idx // 512, idx % 128 // 32])


BF16 = ml_dtypes.bfloat16


def bf(x):
    return np.asarray(x, np.float32).astype(BF16)


def f64(x):
    return np.asarray(x).astype(np.float64)


E2M1 = np.array([0.0, 0.5, 1.0, 1.5, 2.0, 3.0, 4.0, 6.0, -0.0, -0.5, -1.0, -1.5, -2.0, -3.0, -4.0, -6.0])


def pack_weight(w, fmt):
    k, n = w.shape
    w = f64(bf(w)).reshape(k // 32, 32, n)
    amax = np.abs(w).max(1)
    if fmt == "e4m3":
        byte = np.frexp(amax)[1] - 1 + 127 - 7
    else:
        mant, ex = np.frexp(amax / 6.0)
        byte = np.where(mant > 0.5, ex, ex - 1) + 127
    byte = np.clip(np.where(amax > 0, byte, 1), 1, 254)
    scaled = (w * np.exp2(127.0 - byte)[:, None, :]).reshape(k, n).astype(np.float32)
    by_word = np.ascontiguousarray(scaled.reshape(k // 512, 128, 4, n).transpose(0, 1, 3, 2))
    if fmt == "e4m3":
        words = by_word.astype(ml_dtypes.float8_e4m3fn).view(np.uint8)
    else:
        c = by_word.astype(ml_dtypes.float4_e2m1fn).view(np.uint8) & 0xF
        words = c[..., 0::2] | (c[..., 1::2] << 4)
    return np.ascontiguousarray(words), np.ascontiguousarray(byte.astype(np.uint8).reshape(k // 512, 16, n))


def unpack_weight(words, scales, fmt):
    g, p, n, _ = words.shape
    if fmt == "e4m3":
        vals = np.ascontiguousarray(words).view(ml_dtypes.float8_e4m3fn).astype(np.float64)
    else:
        nib = np.empty((g, p, n, 4), np.uint8)
        nib[..., 0::2] = words & 0xF
        nib[..., 1::2] = words >> 4
        vals = E2M1[nib]
    vals = vals * np.repeat(np.exp2(scales.astype(np.float64) - 127.0), 8, axis=1)[..., None]
    return vals.transpose(0, 1, 3, 2).reshape(g * 512, n)

def pack4(w):
    words, scales = pack_weight(w, "e2m1")
    return words.reshape(words.shape[0], 128, -1), scales


def unpack4(words, scales):
    return unpack_weight(words.reshape(words.shape[0], 128, -1, 2), scales, "e2m1")


B, T, D, H, KVH, HD = 2, 512, 2048, 16, 4, 128
HALF = HD // 2
EPS = 1e-6
ROPE_BASE = 10000.0


def zc_rmsnorm(x, scale):
    rms = np.sqrt(np.mean(x ** 2, axis=-1, keepdims=True) + EPS)
    return (1.0 + scale) * x / rms


def apply_rope(x, cos, sin):
    t = x.shape[2]
    c = cos[:t][None, None, :, :]
    s = sin[:t][None, None, :, :]
    x1, x2 = x[..., :HALF], x[..., HALF:]
    return np.concatenate([x1 * c - x2 * s, x2 * c + x1 * s], axis=-1)


def setup_inputs():
    s = mx_kscale(D)
    inv_freq = 1.0 / (ROPE_BASE ** (np.arange(0, HALF) / HALF))
    ang = np.arange(T)[:, None] * inv_freq[None, :]
    kv_input = bf(np.random.standard_normal((B, T, D)) * s)
    Wk_words, Wk_scales = pack4(np.random.standard_normal((D, KVH * HD)) / np.sqrt(D) / s[:, None])
    Wv_words, Wv_scales = pack4(np.random.standard_normal((D, KVH * HD)) / np.sqrt(D) / s[:, None])
    return {"kv_input": kv_input,
            "Wk_words": Wk_words, "Wk_scales": Wk_scales,
            "Wv_words": Wv_words, "Wv_scales": Wv_scales,
            "k_scale": bf(np.random.standard_normal(HD) * 0.2),
            "cos": bf(np.cos(ang)), "sin": bf(np.sin(ang))}


def reference(kv_input, Wk_words, Wk_scales, Wv_words, Wv_scales, k_scale, cos, sin):
    b = kv_input.shape[0]
    xq = mxq(f64(kv_input), 2, "e4m3")
    k = (xq @ unpack4(Wk_words, Wk_scales)).reshape(b, -1, KVH, HD).transpose(0, 2, 1, 3)
    v = (xq @ unpack4(Wv_words, Wv_scales)).reshape(b, -1, KVH, HD).transpose(0, 2, 1, 3)
    k = zc_rmsnorm(k, f64(k_scale))
    rep = H // KVH
    k = np.repeat(k, rep, axis=1)
    v = np.repeat(v, rep, axis=1)
    k = apply_rope(k, f64(cos), f64(sin))
    return k, v

@@ -1,0 +1,197 @@
+from contextlib import ExitStack
+
+import concourse.mybir as mybir
+from concourse.masks import make_identity
+
+F32 = mybir.dt.float32
+BF16 = mybir.dt.bfloat16
+I32 = mybir.dt.int32
+U32 = mybir.dt.uint32
+U8 = mybir.dt.uint8
+FP8X4 = mybir.dt.float8_e4m3fn_x4
+FP4X4 = mybir.dt.float4_e2m1fn_x4
+ACT = mybir.ActivationFunctionType
+
+P = 128
+BATCH = 2
+TOKENS = 512
+D_MODEL = 2048
+KV_HEADS = 4
+HEAD_DIM = 128
+HALF = HEAD_DIM // 2
+REPEAT = 4
+N_OUT = KV_HEADS * HEAD_DIM
+PACK = 4
+K_PASS = P * PACK
+PASSES = D_MODEL // K_PASS
+TILES = TOKENS // P
+EPS = 1e-6
+
+FLOPS = 2 * BATCH * TOKENS * D_MODEL * 2 * N_OUT
+
+
+def load_weight(nc, words_dram, scales_dram, words, planes):
+    for quadrant in range(4):
+        nc.sync.dma_start(
+            out=planes[32 * quadrant : 32 * quadrant + 4].bitcast(I32),
+            in_=scales_dram.bitcast(I32)[:, 4 * quadrant : 4 * quadrant + 4, :].rearrange("g q n -> q g n"),
+        )
+    nc.sync.dma_start(out=words.bitcast(I32), in_=words_dram.bitcast(I32).rearrange("g p n -> p g n"))
+
+
+def store_repeated(nc, out_batch, result):
+    by_copy = out_batch.rearrange("(g r) (p j) d -> r p g (j d)", r=REPEAT, j=TILES)
+    for r in range(REPEAT):
+        nc.sync.dma_start(out=by_copy[r], in_=result.rearrange("p g j d -> p g (j d)"))
+
+
+def tile_multiheadattention_pb_kernel(
+    tc, kv_input, Wk_words, Wk_scales, Wv_words, Wv_scales, k_scale, cos, sin, out_0, out_1
+):
+    nc = tc.nc
+    with ExitStack() as ctx:
+        keep = ctx.enter_context(tc.tile_pool(name="keep", bufs=1))
+        stage = ctx.enter_context(tc.tile_pool(name="stage", bufs=3))
+        psum_t = ctx.enter_context(tc.psum_pool(name="psum_t", bufs=4))
+        psum_mm = ctx.enter_context(tc.psum_pool(name="psum_mm", bufs=4))
+
+        planes = keep.tile([P, 2, PASSES, N_OUT], U8, align_bytes=64)
+        nc.vector.memset(planes[:].bitcast(I32), 0)
+        k_scale_rows = keep.tile([P, HEAD_DIM], BF16)
+        nc.vector.memset(k_scale_rows[:], 0.0)
+        ones = keep.tile([P, P], BF16)
+        nc.vector.memset(ones[:], 1.0)
+        eps = keep.tile([P, 1], F32)
+        nc.vector.memset(eps[:], EPS)
+        ident = keep.tile([P, P], F32)
+        make_identity(nc, ident[:])
+
+        x_sb = [keep.tile([P, TILES, D_MODEL], BF16, name="x_sb%d" % b) for b in range(BATCH)]
+        x_dram = [kv_input[b].rearrange("(p j) k -> p j k", j=TILES) for b in range(BATCH)]
+        wv_words = keep.tile([P, PASSES, 2 * N_OUT], U8, align_bytes=64)
+        wk_words = keep.tile([P, PASSES, 2 * N_OUT], U8, align_bytes=64)
+        cos_sb = keep.tile([P, TILES, HALF], BF16)
+        sin_sb = keep.tile([P, TILES, HALF], BF16)
+
+        nc.sync.dma_start(out=x_sb[0][:, 0, :], in_=x_dram[0][:, 0, :])
+        nc.sync.dma_start(out=x_sb[0][:, 1, :], in_=x_dram[0][:, 1, :])
+        load_weight(nc, Wv_words, Wv_scales, wv_words[:], planes[:, 0])
+        nc.sync.dma_start(out=x_sb[0][:, 2, :], in_=x_dram[0][:, 2, :])
+        nc.sync.dma_start(out=x_sb[0][:, 3, :], in_=x_dram[0][:, 3, :])
+        load_weight(nc, Wk_words, Wk_scales, wk_words[:], planes[:, 1])
+        nc.sync.dma_start(out=k_scale_rows[0:1, :], in_=k_scale.rearrange("(o d) -> o d", o=1))
+        nc.sync.dma_start(out=cos_sb[:], in_=cos.rearrange("(p j) c -> p j c", j=TILES))
+        nc.sync.dma_start(out=sin_sb[:], in_=sin.rearrange("(p j) c -> p j c", j=TILES))
+        nc.sync.dma_start(out=x_sb[1][:], in_=x_dram[1])
+
+        x_codes = keep.tile([P, BATCH, TILES, PASSES * P], U32, align_bytes=64)
+        x_scales = keep.tile([P, BATCH, TILES, PASSES * P], U8, align_bytes=64)
+
+        def quantise_tile(b, j):
+            words = x_sb[b][:, j, :].bitcast(F32)
+            grouped = stage.tile([P, PASSES, P, PACK], BF16, align_bytes=64)
+            grouped_words = grouped[:].bitcast(F32)
+            for bank in range(2):
+                xt = psum_t.tile([P, 2, 2, P], F32)
+                for i in range(2):
+                    g = 2 * bank + i
+                    for u in range(2):
+                        nc.tensor.transpose(
+                            out=xt[:, i, u, :],
+                            in_=words[:, 256 * g + u : 256 * (g + 1) : 2],
+                            identity=ident[:],
+                        )
+                copy = nc.vector.tensor_copy if bank == 0 else nc.scalar.copy
+                copy(out=grouped_words[:, 2 * bank : 2 * bank + 2, :, :], in_=xt[:].rearrange("p g u m -> p g m u"))
+            nc.vector.quantize_mx(
+                out=x_codes[:, b, j, :].bitcast(FP8X4),
+                scales=x_scales[:, b, j, :],
+                in_=grouped[:].rearrange("p g m t -> p (g m t)"),
+            )
+
+        def project(b, j, words, scale_planes):
+            acc = psum_mm.tile([P, KV_HEADS, HEAD_DIM], F32)
+            for g in range(PASSES):
+                cols = slice(g * P, (g + 1) * P)
+                nc.tensor.matmul_mx(
+                    out=acc[:].rearrange("p g d -> p (g d)"),
+                    lhsT=x_codes[:, b, j, cols].bitcast(FP8X4),
+                    lhsT_scale=x_scales[:, b, j, cols],
+                    rhs=words[:, g, :].bitcast(FP4X4),
+                    rhs_scale=scale_planes[:, g, :],
+                    start=(g == 0),
+                    stop=(g == PASSES - 1),
+                )
+            return acc
+
+        table_same = keep.tile([P, TILES, 2, HALF], F32)
+        table_cross = keep.tile([P, TILES, 2, HALF], F32)
+
+        def build_tables():
+            spread = psum_mm.tile([P, HEAD_DIM], F32, tag="acc")
+            nc.tensor.matmul(out=spread[:], lhsT=ones[:], rhs=k_scale_rows[:], start=True, stop=True)
+            gain = keep.tile([P, 2, HALF], F32)
+            nc.vector.tensor_scalar_add(out=gain[:].rearrange("p h c -> p (h c)"), in0=spread[:], scalar1=1.0)
+            signed_gain = keep.tile([P, 2, HALF], F32)
+            nc.vector.tensor_copy(out=signed_gain[:, 0, :], in_=gain[:, 0, :])
+            nc.vector.tensor_scalar_mul(out=signed_gain[:, 1, :], in0=gain[:, 1, :], scalar1=-1.0)
+            shape = [P, TILES, 2, HALF]
+            nc.vector.tensor_mul(
+                out=table_same[:],
+                in0=cos_sb[:].unsqueeze(2).to_broadcast(shape),
+                in1=gain[:].unsqueeze(1).to_broadcast(shape),
+            )
+            nc.vector.tensor_mul(
+                out=table_cross[:],
+                in0=sin_sb[:].unsqueeze(2).to_broadcast(shape),
+                in1=signed_gain[:].unsqueeze(1).to_broadcast(shape),
+            )
+
+        def key_tile(b, j, k_res):
+            acc = project(b, j, wk_words, planes[:, 1])
+            squares = stage.tile([P, KV_HEADS, HEAD_DIM], F32)
+            sum_sq = stage.tile([P, KV_HEADS], F32)
+            for g in range(KV_HEADS):
+                nc.scalar.activation(
+                    out=squares[:, g, :], in_=acc[:, g, :], func=ACT.Square, accum_out=sum_sq[:, g : g + 1]
+                )
+            rms = stage.tile([P, KV_HEADS], F32)
+            nc.scalar.activation(out=rms[:], in_=sum_sq[:], func=ACT.Sqrt, bias=eps[:], scale=1.0 / HEAD_DIM)
+            inv_rms = stage.tile([P, KV_HEADS], F32)
+            nc.vector.reciprocal(out=inv_rms[:], in_=rms[:])
+            normed = stage.tile([P, KV_HEADS, HEAD_DIM], F32)
+            for g in range(KV_HEADS):
+                nc.scalar.activation(
+                    out=normed[:, g, :], in_=acc[:, g, :], func=ACT.Copy, scale=inv_rms[:, g : g + 1]
+                )
+            shape = [P, KV_HEADS, HEAD_DIM]
+            same = stage.tile(shape, F32)
+            cross = stage.tile(shape, F32)
+            nc.vector.tensor_mul(
+                out=same[:],
+                in0=normed[:],
+                in1=table_same[:, j].rearrange("p h c -> p (h c)").unsqueeze(1).to_broadcast(shape),
+            )
+            nc.vector.tensor_mul(
+                out=cross[:],
+                in0=normed[:],
+                in1=table_cross[:, j].rearrange("p h c -> p (h c)").unsqueeze(1).to_broadcast(shape),
+            )
+            nc.vector.tensor_add(out=k_res[:, :, j, 0:HALF], in0=same[:, :, 0:HALF], in1=cross[:, :, HALF:HEAD_DIM])
+            nc.vector.tensor_add(out=k_res[:, :, j, HALF:HEAD_DIM], in0=same[:, :, HALF:HEAD_DIM], in1=cross[:, :, 0:HALF])
+
+        for b in range(BATCH):
+            v_res = keep.tile([P, KV_HEADS, TILES, HEAD_DIM], F32, name="v_res%d" % b)
+            k_res = keep.tile([P, KV_HEADS, TILES, HEAD_DIM], F32, name="k_res%d" % b)
+            quantise_tile(b, 0)
+            for j in range(TILES):
+                if j + 1 < TILES:
+                    quantise_tile(b, j + 1)
+                acc = project(b, j, wv_words, planes[:, 0])
+                nc.scalar.copy(out=v_res[:, :, j, :], in_=acc[:])
+            store_repeated(nc, out_1[b], v_res[:])
+            if b == 0:
+                build_tables()
+            for j in range(TILES):
+                key_tile(b, j, k_res)
+            store_repeated(nc, out_0[b], k_res[:])

@@ -11,6 +11,7 @@ U8 = mybir.dt.uint8
 FP8X4 = mybir.dt.float8_e4m3fn_x4
 FP4X4 = mybir.dt.float4_e2m1fn_x4
 ACT = mybir.ActivationFunctionType
+MULT = mybir.AluOpType.mult
 
 P = 128
 BATCH = 2
@@ -34,15 +35,17 @@ def load_weight(nc, words_dram, scales_dram, words, planes):
     for quadrant in range(4):
         nc.sync.dma_start(
             out=planes[32 * quadrant : 32 * quadrant + 4].bitcast(I32),
-            in_=scales_dram.bitcast(I32)[:, 4 * quadrant : 4 * quadrant + 4, :].rearrange("g q n -> q g n"),
+            in_=scales_dram.bitcast(I32)[:, 4 * quadrant : 4 * quadrant + 4, :].rearrange("c q n -> q c n"),
         )
-    nc.sync.dma_start(out=words.bitcast(I32), in_=words_dram.bitcast(I32).rearrange("g p n -> p g n"))
+    nc.sync.dma_start(out=words.bitcast(I32), in_=words_dram.bitcast(I32).rearrange("c p n -> p c n"))
 
 
-def store_repeated(nc, out_batch, result):
-    by_copy = out_batch.rearrange("(g r) (p j) d -> r p g (j d)", r=REPEAT, j=TILES)
-    for r in range(REPEAT):
-        nc.sync.dma_start(out=by_copy[r], in_=result.rearrange("p g j d -> p g (j d)"))
+def store_head(nc, out_heads, result):
+    row = TILES * HEAD_DIM
+    nc.sync.dma_start(
+        out=out_heads.rearrange("r (p j) d -> p r (j d)", j=TILES),
+        in_=result.rearrange("p j d -> p (j d)").unsqueeze(1).to_broadcast([P, REPEAT, row]),
+    )
 
 
 def tile_multiheadattention_pb_kernel(
@@ -52,9 +55,9 @@ def tile_multiheadattention_pb_kernel(
     with ExitStack() as ctx:
         keep = ctx.enter_context(tc.tile_pool(name="keep", bufs=1))
         stage = ctx.enter_context(tc.tile_pool(name="stage", bufs=3))
+        results = ctx.enter_context(tc.tile_pool(name="results", bufs=BATCH * KV_HEADS))
         psum_t = ctx.enter_context(tc.psum_pool(name="psum_t", bufs=4))
         psum_mm = ctx.enter_context(tc.psum_pool(name="psum_mm", bufs=4))
-
         planes = keep.tile([P, 2, PASSES, N_OUT], U8, align_bytes=64)
         nc.vector.memset(planes[:].bitcast(I32), 0)
         k_scale_rows = keep.tile([P, HEAD_DIM], BF16)
@@ -66,62 +69,66 @@ def tile_multiheadattention_pb_kernel(
         ident = keep.tile([P, P], F32)
         make_identity(nc, ident[:])
 
-        x_sb = [keep.tile([P, TILES, D_MODEL], BF16, name="x_sb%d" % b) for b in range(BATCH)]
-        x_dram = [kv_input[b].rearrange("(p j) k -> p j k", j=TILES) for b in range(BATCH)]
+        x_sb = keep.tile([P, BATCH, TILES, D_MODEL], BF16)
         wv_words = keep.tile([P, PASSES, 2 * N_OUT], U8, align_bytes=64)
         wk_words = keep.tile([P, PASSES, 2 * N_OUT], U8, align_bytes=64)
         cos_sb = keep.tile([P, TILES, HALF], BF16)
         sin_sb = keep.tile([P, TILES, HALF], BF16)
 
-        nc.sync.dma_start(out=x_sb[0][:, 0, :], in_=x_dram[0][:, 0, :])
-        nc.sync.dma_start(out=x_sb[0][:, 1, :], in_=x_dram[0][:, 1, :])
+        def load_tokens(b, j):
+            nc.sync.dma_start(out=x_sb[:, b, j, :], in_=kv_input[b].rearrange("(p j) k -> p j k", j=TILES)[:, j, :])
+
+        load_tokens(0, 0)
+        load_tokens(0, 1)
         load_weight(nc, Wv_words, Wv_scales, wv_words[:], planes[:, 0])
-        nc.sync.dma_start(out=x_sb[0][:, 2, :], in_=x_dram[0][:, 2, :])
-        nc.sync.dma_start(out=x_sb[0][:, 3, :], in_=x_dram[0][:, 3, :])
+        load_tokens(0, 2)
+        load_tokens(0, 3)
         load_weight(nc, Wk_words, Wk_scales, wk_words[:], planes[:, 1])
         nc.sync.dma_start(out=k_scale_rows[0:1, :], in_=k_scale.rearrange("(o d) -> o d", o=1))
         nc.sync.dma_start(out=cos_sb[:], in_=cos.rearrange("(p j) c -> p j c", j=TILES))
         nc.sync.dma_start(out=sin_sb[:], in_=sin.rearrange("(p j) c -> p j c", j=TILES))
-        nc.sync.dma_start(out=x_sb[1][:], in_=x_dram[1])
+        for j in range(TILES):
+            load_tokens(1, j)
 
         x_codes = keep.tile([P, BATCH, TILES, PASSES * P], U32, align_bytes=64)
         x_scales = keep.tile([P, BATCH, TILES, PASSES * P], U8, align_bytes=64)
 
         def quantise_tile(b, j):
-            words = x_sb[b][:, j, :].bitcast(F32)
+            words = x_sb[:, b, j, :].bitcast(F32)
             grouped = stage.tile([P, PASSES, P, PACK], BF16, align_bytes=64)
             grouped_words = grouped[:].bitcast(F32)
             for bank in range(2):
                 xt = psum_t.tile([P, 2, 2, P], F32)
                 for i in range(2):
-                    g = 2 * bank + i
+                    c = 2 * bank + i
                     for u in range(2):
                         nc.tensor.transpose(
                             out=xt[:, i, u, :],
-                            in_=words[:, 256 * g + u : 256 * (g + 1) : 2],
+                            in_=words[:, 256 * c + u : 256 * (c + 1) : 2],
                             identity=ident[:],
                         )
-                copy = nc.vector.tensor_copy if bank == 0 else nc.scalar.copy
-                copy(out=grouped_words[:, 2 * bank : 2 * bank + 2, :, :], in_=xt[:].rearrange("p g u m -> p g m u"))
+                nc.scalar.copy(
+                    out=grouped_words[:, 2 * bank : 2 * bank + 2, :, :], in_=xt[:].rearrange("p c u m -> p c m u")
+                )
             nc.vector.quantize_mx(
                 out=x_codes[:, b, j, :].bitcast(FP8X4),
                 scales=x_scales[:, b, j, :],
-                in_=grouped[:].rearrange("p g m t -> p (g m t)"),
+                in_=grouped[:].rearrange("p c m t -> p (c m t)"),
             )
 
-        def project(b, j, words, scale_planes):
-            acc = psum_mm.tile([P, KV_HEADS, HEAD_DIM], F32)
-            for g in range(PASSES):
-                cols = slice(g * P, (g + 1) * P)
-                nc.tensor.matmul_mx(
-                    out=acc[:].rearrange("p g d -> p (g d)"),
-                    lhsT=x_codes[:, b, j, cols].bitcast(FP8X4),
-                    lhsT_scale=x_scales[:, b, j, cols],
-                    rhs=words[:, g, :].bitcast(FP4X4),
-                    rhs_scale=scale_planes[:, g, :],
-                    start=(g == 0),
-                    stop=(g == PASSES - 1),
-                )
+        def project(b, g, words, scale_planes):
+            acc = psum_mm.tile([P, TILES, HEAD_DIM], F32)
+            for j in range(TILES):
+                for c in range(PASSES):
+                    nc.tensor.matmul_mx(
+                        out=acc[:, j, :],
+                        lhsT=x_codes[:, b, j, c * P : (c + 1) * P].bitcast(FP8X4),
+                        lhsT_scale=x_scales[:, b, j, c * P : (c + 1) * P],
+                        rhs=words[:, c, 2 * HEAD_DIM * g : 2 * HEAD_DIM * (g + 1)].bitcast(FP4X4),
+                        rhs_scale=scale_planes[:, c, HEAD_DIM * g : HEAD_DIM * (g + 1)],
+                        start=(c == 0),
+                        stop=(c == PASSES - 1),
+                    )
             return acc
 
         table_same = keep.tile([P, TILES, 2, HALF], F32)
@@ -147,51 +154,48 @@ def tile_multiheadattention_pb_kernel(
                 in1=signed_gain[:].unsqueeze(1).to_broadcast(shape),
             )
 
-        def key_tile(b, j, k_res):
-            acc = project(b, j, wk_words, planes[:, 1])
-            squares = stage.tile([P, KV_HEADS, HEAD_DIM], F32)
-            sum_sq = stage.tile([P, KV_HEADS], F32)
-            for g in range(KV_HEADS):
-                nc.scalar.activation(
-                    out=squares[:, g, :], in_=acc[:, g, :], func=ACT.Square, accum_out=sum_sq[:, g : g + 1]
-                )
-            rms = stage.tile([P, KV_HEADS], F32)
-            nc.scalar.activation(out=rms[:], in_=sum_sq[:], func=ACT.Sqrt, bias=eps[:], scale=1.0 / HEAD_DIM)
-            inv_rms = stage.tile([P, KV_HEADS], F32)
-            nc.vector.reciprocal(out=inv_rms[:], in_=rms[:])
-            normed = stage.tile([P, KV_HEADS, HEAD_DIM], F32)
-            for g in range(KV_HEADS):
-                nc.scalar.activation(
-                    out=normed[:, g, :], in_=acc[:, g, :], func=ACT.Copy, scale=inv_rms[:, g : g + 1]
-                )
-            shape = [P, KV_HEADS, HEAD_DIM]
-            same = stage.tile(shape, F32)
-            cross = stage.tile(shape, F32)
-            nc.vector.tensor_mul(
-                out=same[:],
-                in0=normed[:],
-                in1=table_same[:, j].rearrange("p h c -> p (h c)").unsqueeze(1).to_broadcast(shape),
-            )
-            nc.vector.tensor_mul(
-                out=cross[:],
-                in0=normed[:],
-                in1=table_cross[:, j].rearrange("p h c -> p (h c)").unsqueeze(1).to_broadcast(shape),
-            )
-            nc.vector.tensor_add(out=k_res[:, :, j, 0:HALF], in0=same[:, :, 0:HALF], in1=cross[:, :, HALF:HEAD_DIM])
-            nc.vector.tensor_add(out=k_res[:, :, j, HALF:HEAD_DIM], in0=same[:, :, HALF:HEAD_DIM], in1=cross[:, :, 0:HALF])
+        def value_head(b, g):
+            acc = project(b, g, wv_words, planes[:, 0])
+            v_res = results.tile([P, TILES, HEAD_DIM], F32)
+            nc.scalar.copy(out=v_res[:], in_=acc[:])
+            store_head(nc, out_1[b, REPEAT * g : REPEAT * (g + 1)], v_res[:])
 
+        def key_head(b, g):
+            acc = project(b, g, wk_words, planes[:, 1])
+            squares = stage.tile([P, TILES, HEAD_DIM], F32)
+            sum_sq = stage.tile([P, TILES], F32)
+            for j in range(TILES):
+                nc.scalar.activation(
+                    out=squares[:, j, :], in_=acc[:, j, :], func=ACT.Square, accum_out=sum_sq[:, j : j + 1]
+                )
+            rms = stage.tile([P, TILES], F32)
+            nc.scalar.activation(out=rms[:], in_=sum_sq[:], func=ACT.Sqrt, bias=eps[:], scale=1.0 / HEAD_DIM)
+            inv_rms = stage.tile([P, TILES], F32)
+            nc.vector.reciprocal(out=inv_rms[:], in_=rms[:])
+            same = stage.tile([P, TILES, HEAD_DIM], F32)
+            cross = stage.tile([P, TILES, HEAD_DIM], F32)
+            for j in range(TILES):
+                for product, table in ((same, table_same), (cross, table_cross)):
+                    nc.vector.scalar_tensor_tensor(
+                        out=product[:, j, :],
+                        in0=acc[:, j, :],
+                        scalar=inv_rms[:, j : j + 1],
+                        in1=table[:, j].rearrange("p h c -> p (h c)"),
+                        op0=MULT,
+                        op1=MULT,
+                    )
+            k_res = results.tile([P, TILES, HEAD_DIM], F32)
+            nc.vector.tensor_add(out=k_res[:, :, 0:HALF], in0=same[:, :, 0:HALF], in1=cross[:, :, HALF:HEAD_DIM])
+            nc.vector.tensor_add(out=k_res[:, :, HALF:HEAD_DIM], in0=same[:, :, HALF:HEAD_DIM], in1=cross[:, :, 0:HALF])
+            store_head(nc, out_0[b, REPEAT * g : REPEAT * (g + 1)], k_res[:])
+
+        for j in range(TILES):
+            quantise_tile(0, j)
         for b in range(BATCH):
-            v_res = keep.tile([P, KV_HEADS, TILES, HEAD_DIM], F32, name="v_res%d" % b)
-            k_res = keep.tile([P, KV_HEADS, TILES, HEAD_DIM], F32, name="k_res%d" % b)
-            quantise_tile(b, 0)
-            for j in range(TILES):
-                if j + 1 < TILES:
-                    quantise_tile(b, j + 1)
-                acc = project(b, j, wv_words, planes[:, 0])
-                nc.scalar.copy(out=v_res[:, :, j, :], in_=acc[:])
-            store_repeated(nc, out_1[b], v_res[:])
-            if b == 0:
-                build_tables()
-            for j in range(TILES):
-                key_tile(b, j, k_res)
-            store_repeated(nc, out_0[b], k_res[:])
+            for g in range(KV_HEADS):
+                value_head(b, g)
+                if b == 0 and g == 0:
+                    build_tables()
+                key_head(b, g)
+                if b + 1 < BATCH:
+                    quantise_tile(b + 1, g)

@@ -31,12 +31,15 @@ EPS = 1e-6
 FLOPS = 2 * BATCH * TOKENS * D_MODEL * 2 * N_OUT
 
 
-def load_weight(nc, words_dram, scales_dram, words, planes):
+def load_scales(nc, scales_dram, planes):
     for quadrant in range(4):
         nc.sync.dma_start(
             out=planes[32 * quadrant : 32 * quadrant + 4].bitcast(I32),
             in_=scales_dram.bitcast(I32)[:, 4 * quadrant : 4 * quadrant + 4, :].rearrange("c q n -> q c n"),
         )
+
+
+def load_words(nc, words_dram, words):
     nc.sync.dma_start(out=words.bitcast(I32), in_=words_dram.bitcast(I32).rearrange("c p n -> p c n"))
 
 
@@ -58,6 +61,7 @@ def tile_multiheadattention_pb_kernel(
         results = ctx.enter_context(tc.tile_pool(name="results", bufs=BATCH * KV_HEADS))
         psum_t = ctx.enter_context(tc.psum_pool(name="psum_t", bufs=4))
         psum_mm = ctx.enter_context(tc.psum_pool(name="psum_mm", bufs=4))
+        ctx.enter_context(tc.manual_schedule())
         planes = keep.tile([P, 2, PASSES, N_OUT], U8, align_bytes=64)
         nc.vector.memset(planes[:].bitcast(I32), 0)
         k_scale_rows = keep.tile([P, HEAD_DIM], BF16)
@@ -75,20 +79,17 @@ def tile_multiheadattention_pb_kernel(
         cos_sb = keep.tile([P, TILES, HALF], BF16)
         sin_sb = keep.tile([P, TILES, HALF], BF16)
 
-        def load_tokens(b, j):
-            nc.sync.dma_start(out=x_sb[:, b, j, :], in_=kv_input[b].rearrange("(p j) k -> p j k", j=TILES)[:, j, :])
-
-        load_tokens(0, 0)
-        load_tokens(0, 1)
-        load_weight(nc, Wv_words, Wv_scales, wv_words[:], planes[:, 0])
-        load_tokens(0, 2)
-        load_tokens(0, 3)
-        load_weight(nc, Wk_words, Wk_scales, wk_words[:], planes[:, 1])
-        nc.sync.dma_start(out=k_scale_rows[0:1, :], in_=k_scale.rearrange("(o d) -> o d", o=1))
-        nc.sync.dma_start(out=cos_sb[:], in_=cos.rearrange("(p j) c -> p j c", j=TILES))
-        nc.sync.dma_start(out=sin_sb[:], in_=sin.rearrange("(p j) c -> p j c", j=TILES))
+        x_dram = kv_input.rearrange("b (p j) k -> b p j k", j=TILES)
         for j in range(TILES):
-            load_tokens(1, j)
+            nc.sync.dma_start(out=x_sb[:, 0, j, :], in_=x_dram[0, :, j, :])
+        load_scales(nc, Wv_scales, planes[:, 0])
+        load_words(nc, Wv_words, wv_words[:])
+        nc.sync.dma_start(out=x_sb[:, 1], in_=x_dram[1])
+        load_words(nc, Wk_words, wk_words[:])
+        load_scales(nc, Wk_scales, planes[:, 1])
+        nc.gpsimd.dma_start(out=k_scale_rows[0:1, :], in_=k_scale.rearrange("(o d) -> o d", o=1))
+        nc.gpsimd.dma_start(out=cos_sb[:], in_=cos.rearrange("(p j) c -> p j c", j=TILES))
+        nc.gpsimd.dma_start(out=sin_sb[:], in_=sin.rearrange("(p j) c -> p j c", j=TILES))
 
         x_codes = keep.tile([P, BATCH, TILES, PASSES * P], U32, align_bytes=64)
         x_scales = keep.tile([P, BATCH, TILES, PASSES * P], U8, align_bytes=64)
@@ -194,8 +195,9 @@ def tile_multiheadattention_pb_kernel(
         for b in range(BATCH):
             for g in range(KV_HEADS):
                 value_head(b, g)
-                if b == 0 and g == 0:
-                    build_tables()
+            if b == 0:
+                build_tables()
+            for g in range(KV_HEADS):
                 key_head(b, g)
                 if b + 1 < BATCH:
                     quantise_tile(b + 1, g)

@@ -44,11 +44,10 @@ def load_words(nc, words_dram, words):
 
 
 def store_head(nc, out_heads, result):
-    row = TILES * HEAD_DIM
-    nc.sync.dma_start(
-        out=out_heads.rearrange("r (p j) d -> p r (j d)", j=TILES),
-        in_=result.rearrange("p j d -> p (j d)").unsqueeze(1).to_broadcast([P, REPEAT, row]),
-    )
+    for r in range(REPEAT):
+        nc.sync.dma_start(
+            out=out_heads[r].rearrange("(p j) d -> p (j d)", j=TILES), in_=result.rearrange("p j d -> p (j d)")
+        )
 
 
 def tile_multiheadattention_pb_kernel(

@@ -32,10 +32,10 @@ FLOPS = 2 * BATCH * TOKENS * D_MODEL * 2 * N_OUT
 
 
 def load_scales(nc, scales_dram, planes):
-    for quadrant in range(4):
+    for r in range(4):
         nc.sync.dma_start(
-            out=planes[32 * quadrant : 32 * quadrant + 4].bitcast(I32),
-            in_=scales_dram.bitcast(I32)[:, 4 * quadrant : 4 * quadrant + 4, :].rearrange("c q n -> q c n"),
+            out=planes[r:P:32].bitcast(I32),
+            in_=scales_dram.bitcast(I32)[:, r:16:4, :].rearrange("c q n -> q c n"),
         )
 
 
@@ -44,10 +44,11 @@ def load_words(nc, words_dram, words):
 
 
 def store_head(nc, out_heads, result):
-    for r in range(REPEAT):
-        nc.sync.dma_start(
-            out=out_heads[r].rearrange("(p j) d -> p (j d)", j=TILES), in_=result.rearrange("p j d -> p (j d)")
-        )
+    row = TILES * HEAD_DIM
+    nc.sync.dma_start(
+        out=out_heads.rearrange("r (p j) d -> p r (j d)", j=TILES),
+        in_=result.rearrange("p j d -> p (j d)").unsqueeze(1).to_broadcast([P, REPEAT, row]),
+    )
 
 
 def tile_multiheadattention_pb_kernel(

@@ -62,14 +62,16 @@ def tile_multiheadattention_pb_kernel(
         psum_t = ctx.enter_context(tc.psum_pool(name="psum_t", bufs=4))
         psum_mm = ctx.enter_context(tc.psum_pool(name="psum_mm", bufs=4))
         ctx.enter_context(tc.manual_schedule())
+        eps = keep.tile([P, 1], F32)
+        nc.vector.memset(eps[:], EPS)
+        warm = keep.tile([P, 1], F32)
+        nc.scalar.activation(out=warm[:], in_=eps[:], func=ACT.Sqrt)
         planes = keep.tile([P, 2, PASSES, N_OUT], U8, align_bytes=64)
         nc.vector.memset(planes[:].bitcast(I32), 0)
         k_scale_rows = keep.tile([P, HEAD_DIM], BF16)
         nc.vector.memset(k_scale_rows[:], 0.0)
         ones = keep.tile([P, P], BF16)
         nc.vector.memset(ones[:], 1.0)
-        eps = keep.tile([P, 1], F32)
-        nc.vector.memset(eps[:], EPS)
         ident = keep.tile([P, P], F32)
         make_identity(nc, ident[:])
 

from contextlib import ExitStack

import concourse.mybir as mybir
from concourse.masks import make_identity

F32 = mybir.dt.float32
BF16 = mybir.dt.bfloat16
I32 = mybir.dt.int32
U32 = mybir.dt.uint32
U8 = mybir.dt.uint8
FP8X4 = mybir.dt.float8_e4m3fn_x4
FP4X4 = mybir.dt.float4_e2m1fn_x4
ACT = mybir.ActivationFunctionType
MULT = mybir.AluOpType.mult

P = 128
BATCH = 2
TOKENS = 512
D_MODEL = 2048
KV_HEADS = 4
HEAD_DIM = 128
HALF = HEAD_DIM // 2
REPEAT = 4
N_OUT = KV_HEADS * HEAD_DIM
PACK = 4
K_PASS = P * PACK
PASSES = D_MODEL // K_PASS
TILES = TOKENS // P
EPS = 1e-6

FLOPS = 2 * BATCH * TOKENS * D_MODEL * 2 * N_OUT


def load_scales(nc, scales_dram, planes):
    for r in range(4):
        nc.sync.dma_start(
            out=planes[r:P:32].bitcast(I32),
            in_=scales_dram.bitcast(I32)[:, r:16:4, :].rearrange("c q n -> q c n"),
        )


def load_words(nc, words_dram, words):
    nc.sync.dma_start(out=words.bitcast(I32), in_=words_dram.bitcast(I32).rearrange("c p n -> p c n"))


def store_head(nc, out_heads, result):
    row = TILES * HEAD_DIM
    nc.sync.dma_start(
        out=out_heads.rearrange("r (p j) d -> p r (j d)", j=TILES),
        in_=result.rearrange("p j d -> p (j d)").unsqueeze(1).to_broadcast([P, REPEAT, row]),
    )


def tile_multiheadattention_pb_kernel(
    tc, kv_input, Wk_words, Wk_scales, Wv_words, Wv_scales, k_scale, cos, sin, out_0, out_1
):
    nc = tc.nc
    with ExitStack() as ctx:
        keep = ctx.enter_context(tc.tile_pool(name="keep", bufs=1))
        stage = ctx.enter_context(tc.tile_pool(name="stage", bufs=3))
        results = ctx.enter_context(tc.tile_pool(name="results", bufs=BATCH * KV_HEADS))
        psum_t = ctx.enter_context(tc.psum_pool(name="psum_t", bufs=4))
        psum_mm = ctx.enter_context(tc.psum_pool(name="psum_mm", bufs=4))
        ctx.enter_context(tc.manual_schedule())
        eps = keep.tile([P, 1], F32)
        nc.vector.memset(eps[:], EPS)
        warm = keep.tile([P, 1], F32)
        nc.scalar.activation(out=warm[:], in_=eps[:], func=ACT.Sqrt)
        planes = keep.tile([P, 2, PASSES, N_OUT], U8, align_bytes=64)
        nc.vector.memset(planes[:].bitcast(I32), 0)
        k_scale_rows = keep.tile([P, HEAD_DIM], BF16)
        nc.vector.memset(k_scale_rows[:], 0.0)
        ones = keep.tile([P, P], BF16)
        nc.vector.memset(ones[:], 1.0)
        ident = keep.tile([P, P], F32)
        make_identity(nc, ident[:])

        x_sb = keep.tile([P, BATCH, TILES, D_MODEL], BF16)
        wv_words = keep.tile([P, PASSES, 2 * N_OUT], U8, align_bytes=64)
        wk_words = keep.tile([P, PASSES, 2 * N_OUT], U8, align_bytes=64)
        cos_sb = keep.tile([P, TILES, HALF], BF16)
        sin_sb = keep.tile([P, TILES, HALF], BF16)

        x_dram = kv_input.rearrange("b (p j) k -> b p j k", j=TILES)
        for j in range(TILES):
            nc.sync.dma_start(out=x_sb[:, 0, j, :], in_=x_dram[0, :, j, :])
        load_scales(nc, Wv_scales, planes[:, 0])
        load_words(nc, Wv_words, wv_words[:])
        nc.sync.dma_start(out=x_sb[:, 1], in_=x_dram[1])
        load_words(nc, Wk_words, wk_words[:])
        load_scales(nc, Wk_scales, planes[:, 1])
        nc.gpsimd.dma_start(out=k_scale_rows[0:1, :], in_=k_scale.rearrange("(o d) -> o d", o=1))
        nc.gpsimd.dma_start(out=cos_sb[:], in_=cos.rearrange("(p j) c -> p j c", j=TILES))
        nc.gpsimd.dma_start(out=sin_sb[:], in_=sin.rearrange("(p j) c -> p j c", j=TILES))

        x_codes = keep.tile([P, BATCH, TILES, PASSES * P], U32, align_bytes=64)
        x_scales = keep.tile([P, BATCH, TILES, PASSES * P], U8, align_bytes=64)

        def quantise_tile(b, j):
            words = x_sb[:, b, j, :].bitcast(F32)
            grouped = stage.tile([P, PASSES, P, PACK], BF16, align_bytes=64)
            grouped_words = grouped[:].bitcast(F32)
            for bank in range(2):
                xt = psum_t.tile([P, 2, 2, P], F32)
                for i in range(2):
                    c = 2 * bank + i
                    for u in range(2):
                        nc.tensor.transpose(
                            out=xt[:, i, u, :],
                            in_=words[:, 256 * c + u : 256 * (c + 1) : 2],
                            identity=ident[:],
                        )
                nc.scalar.copy(
                    out=grouped_words[:, 2 * bank : 2 * bank + 2, :, :], in_=xt[:].rearrange("p c u m -> p c m u")
                )
            nc.vector.quantize_mx(
                out=x_codes[:, b, j, :].bitcast(FP8X4),
                scales=x_scales[:, b, j, :],
                in_=grouped[:].rearrange("p c m t -> p (c m t)"),
            )

        def project(b, g, words, scale_planes):
            acc = psum_mm.tile([P, TILES, HEAD_DIM], F32)
            for j in range(TILES):
                for c in range(PASSES):
                    nc.tensor.matmul_mx(
                        out=acc[:, j, :],
                        lhsT=x_codes[:, b, j, c * P : (c + 1) * P].bitcast(FP8X4),
                        lhsT_scale=x_scales[:, b, j, c * P : (c + 1) * P],
                        rhs=words[:, c, 2 * HEAD_DIM * g : 2 * HEAD_DIM * (g + 1)].bitcast(FP4X4),
                        rhs_scale=scale_planes[:, c, HEAD_DIM * g : HEAD_DIM * (g + 1)],
                        start=(c == 0),
                        stop=(c == PASSES - 1),
                    )
            return acc

        table_same = keep.tile([P, TILES, 2, HALF], F32)
        table_cross = keep.tile([P, TILES, 2, HALF], F32)

        def build_tables():
            spread = psum_mm.tile([P, HEAD_DIM], F32, tag="acc")
            nc.tensor.matmul(out=spread[:], lhsT=ones[:], rhs=k_scale_rows[:], start=True, stop=True)
            gain = keep.tile([P, 2, HALF], F32)
            nc.vector.tensor_scalar_add(out=gain[:].rearrange("p h c -> p (h c)"), in0=spread[:], scalar1=1.0)
            signed_gain = keep.tile([P, 2, HALF], F32)
            nc.vector.tensor_copy(out=signed_gain[:, 0, :], in_=gain[:, 0, :])
            nc.vector.tensor_scalar_mul(out=signed_gain[:, 1, :], in0=gain[:, 1, :], scalar1=-1.0)
            shape = [P, TILES, 2, HALF]
            nc.vector.tensor_mul(
                out=table_same[:],
                in0=cos_sb[:].unsqueeze(2).to_broadcast(shape),
                in1=gain[:].unsqueeze(1).to_broadcast(shape),
            )
            nc.vector.tensor_mul(
                out=table_cross[:],
                in0=sin_sb[:].unsqueeze(2).to_broadcast(shape),
                in1=signed_gain[:].unsqueeze(1).to_broadcast(shape),
            )

        def value_head(b, g):
            acc = project(b, g, wv_words, planes[:, 0])
            v_res = results.tile([P, TILES, HEAD_DIM], F32)
            nc.scalar.copy(out=v_res[:], in_=acc[:])
            store_head(nc, out_1[b, REPEAT * g : REPEAT * (g + 1)], v_res[:])

        def key_head(b, g):
            acc = project(b, g, wk_words, planes[:, 1])
            squares = stage.tile([P, TILES, HEAD_DIM], F32)
            sum_sq = stage.tile([P, TILES], F32)
            for j in range(TILES):
                nc.scalar.activation(
                    out=squares[:, j, :], in_=acc[:, j, :], func=ACT.Square, accum_out=sum_sq[:, j : j + 1]
                )
            rms = stage.tile([P, TILES], F32)
            nc.scalar.activation(out=rms[:], in_=sum_sq[:], func=ACT.Sqrt, bias=eps[:], scale=1.0 / HEAD_DIM)
            inv_rms = stage.tile([P, TILES], F32)
            nc.vector.reciprocal(out=inv_rms[:], in_=rms[:])
            same = stage.tile([P, TILES, HEAD_DIM], F32)
            cross = stage.tile([P, TILES, HEAD_DIM], F32)
            for j in range(TILES):
                for product, table in ((same, table_same), (cross, table_cross)):
                    nc.vector.scalar_tensor_tensor(
                        out=product[:, j, :],
                        in0=acc[:, j, :],
                        scalar=inv_rms[:, j : j + 1],
                        in1=table[:, j].rearrange("p h c -> p (h c)"),
                        op0=MULT,
                        op1=MULT,
                    )
            k_res = results.tile([P, TILES, HEAD_DIM], F32)
            nc.vector.tensor_add(out=k_res[:, :, 0:HALF], in0=same[:, :, 0:HALF], in1=cross[:, :, HALF:HEAD_DIM])
            nc.vector.tensor_add(out=k_res[:, :, HALF:HEAD_DIM], in0=same[:, :, HALF:HEAD_DIM], in1=cross[:, :, 0:HALF])
            store_head(nc, out_0[b, REPEAT * g : REPEAT * (g + 1)], k_res[:])

        for j in range(TILES):
            quantise_tile(0, j)
        for b in range(BATCH):
            for g in range(KV_HEADS):
                value_head(b, g)
            if b == 0:
                build_tables()
            for g in range(KV_HEADS):
                key_head(b, g)
                if b + 1 < BATCH:
                    quantise_tile(b + 1, g)
